import numpy as np
import ml_dtypes

BF16 = ml_dtypes.bfloat16


def bf(x):
    return np.asarray(x, np.float32).astype(BF16)


def f32(x):
    return np.asarray(x, np.float32)


def f64(x):
    return np.asarray(x).astype(np.float64)


def striped(idx):
    return np.tile(idx.reshape(-1, 16).T, (8, 1))


D, D3, S, N, H, DH = 512, 1536, 2048, 1024, 4, 128
EPS = 1e-5


def setup_inputs():
    return {
        "embed": f32(np.random.standard_normal((D, S))),
        "pos": f32(0.5 * np.random.standard_normal((D, N))),
        "ln_w": f32(1.0 + 0.1 * np.random.standard_normal((D, 1))),
        "ln_b": f32(0.1 * np.random.standard_normal((D, 1))),
        "w_attn": bf(1.5 * np.random.standard_normal((D, D3)) / np.sqrt(D)),
        "b_attn": f32(0.1 * np.random.standard_normal((D3, 1))),
        "w_o": bf(1.5 * np.random.standard_normal((D, D)) / np.sqrt(D)),
        "b_o": f32(0.1 * np.random.standard_normal((D, 1))),
        "offs": striped(np.random.permutation(np.tile(np.arange(S), 2))[:N]),
    }


def reference(embed, pos, ln_w, ln_b, w_attn, b_attn, w_o, b_o, offs):
    idx = offs[:16].T.reshape(-1)
    res = f64(embed)[:, idx] + f64(pos)
    mu = res.mean(axis=0, keepdims=True)
    sd = np.sqrt(((res - mu) ** 2).mean(axis=0, keepdims=True))
    x = f64(ln_w) * ((res - mu) / (sd + EPS)) + f64(ln_b)
    qkv = f64(w_attn).T @ x + f64(b_attn)
    q = qkv[:D].reshape(H, DH, N)
    k = qkv[D:D + D].reshape(H, DH, N)
    v = qkv[D + D:].reshape(H, DH, N)
    keep = np.arange(N)[:, None] <= np.arange(N)[None, :]
    att = np.zeros((H, DH, N), np.float64)
    for h in range(H):
        sc = np.where(keep, k[h].T @ q[h] / np.sqrt(DH), -np.inf)
        e = np.exp(sc - sc.max(axis=0, keepdims=True))
        p = e / e.sum(axis=0, keepdims=True)
        att[h] = v[h] @ p
    return f64(w_o).T @ att.reshape(D, N) + f64(b_o) + res

@@ -1,0 +1,285 @@
+import math
+from contextlib import ExitStack
+
+import concourse.mybir as mybir
+from concourse.masks import make_identity
+
+F32 = mybir.dt.float32
+BF16 = mybir.dt.bfloat16
+U16 = mybir.dt.uint16
+I32 = mybir.dt.int32
+ALU = mybir.AluOpType
+FUNC = mybir.ActivationFunctionType
+AXIS = mybir.AxisListType
+
+P = 128
+D = 512
+S = 2048
+N = 1024
+HEADS = 4
+EPS = 1e-5
+CHANNEL_BLOCKS = D // P
+CHUNK = 512
+CHUNKS = N // CHUNK
+BLOCKS_PER_CHUNK = CHUNK // P
+SCORE_SCALE = 1.0 / math.sqrt(P)
+MASKED = -1.0e30
+
+ROW_LN_W = 0
+ROW_LN_B = ROW_LN_W + CHANNEL_BLOCKS
+ROW_B_O = ROW_LN_B + CHANNEL_BLOCKS
+ROW_B_QK = ROW_B_O + CHANNEL_BLOCKS
+ROWS_USED = ROW_B_QK + 2 * CHANNEL_BLOCKS
+
+FLOPS = 2 * D * 3 * D * N + 2 * D * D * N + 2 * (2 * D * N * (N + 1) // 2)
+
+
+def block(i):
+    return slice(i * P, (i + 1) * P)
+
+
+def tile_jtransformer_b_kernel(
+    tc, embed, pos, ln_w, ln_b, w_attn, b_attn, w_o, b_o, offs, out
+):
+    nc = tc.nc
+    with ExitStack() as stack:
+        held = stack.enter_context(tc.tile_pool(name="held", bufs=1))
+        work = stack.enter_context(tc.tile_pool(name="work", bufs=2))
+        small = stack.enter_context(tc.tile_pool(name="small", bufs=4))
+        token_banks = stack.enter_context(tc.psum_pool(name="token_banks", bufs=4))
+        flip_banks = stack.enter_context(tc.psum_pool(name="flip_banks", bufs=2))
+        product_banks = stack.enter_context(tc.psum_pool(name="product_banks", bufs=2))
+
+        offsets = held.tile([P, N // 16], U16, name="offsets")
+        nc.sync.dma_start(offsets[:], offs)
+
+        rows = held.tile([P, P], F32, name="rows")
+        nc.gpsimd.memset(rows[:], 0.0)
+        for first_row, vector in (
+            (ROW_LN_W, ln_w),
+            (ROW_LN_B, ln_b),
+            (ROW_B_O, b_o),
+            (ROW_B_QK, b_attn[0 : 2 * D, :]),
+        ):
+            as_rows = vector.rearrange("(r c) o -> r (c o)", c=P)
+            nc.scalar.dma_start(rows[first_row : first_row + as_rows.shape[0], :], as_rows)
+
+        table = [held.tile([P, S], F32, name=f"table{b}") for b in range(CHANNEL_BLOCKS)]
+        pos_sb = [held.tile([P, N], F32, name=f"pos_sb{b}") for b in range(CHANNEL_BLOCKS)]
+        for b in range(CHANNEL_BLOCKS):
+            nc.sync.dma_start(table[b][:], embed[block(b), :])
+            nc.sync.dma_start(pos_sb[b][:, 0:CHUNK], pos[block(b), 0:CHUNK])
+        for b in range(CHANNEL_BLOCKS):
+            nc.sync.dma_start(pos_sb[b][:, CHUNK:N], pos[block(b), CHUNK:N])
+        w_attn_sb = [held.tile([P, 3 * D], BF16, name=f"w_attn_sb{b}") for b in range(CHANNEL_BLOCKS)]
+        for b in range(CHANNEL_BLOCKS):
+            nc.sync.dma_start(w_attn_sb[b][:], w_attn[block(b), :])
+        b_v_all = held.tile([P, D], F32, name="b_v_all")
+        nc.sync.dma_start(
+            b_v_all[:], b_attn[2 * D : 3 * D, :].rearrange("e o -> (e o)").partition_broadcast(P)
+        )
+        w_o_sb = [held.tile([P, D], BF16, name=f"w_o_sb{b}") for b in range(CHANNEL_BLOCKS)]
+        for b in range(CHANNEL_BLOCKS):
+            nc.sync.dma_start(w_o_sb[b][:], w_o[block(b), :])
+
+        ident_f32 = held.tile([P, P], F32, name="ident_f32")
+        make_identity(nc, ident_f32[:])
+        ident_bf16 = held.tile([P, P], BF16, name="ident_bf16")
+        make_identity(nc, ident_bf16[:])
+        key_minus_query = held.tile([P, P], I32, name="key_minus_query")
+        nc.gpsimd.iota(key_minus_query[:], pattern=[[1, P]], base=0, channel_multiplier=-1)
+        causal = held.tile([P, P], BF16, name="causal")
+        nc.vector.tensor_scalar(causal[:], key_minus_query[:], 0.0, MASKED, ALU.is_gt, ALU.mult)
+
+        columns_ps = flip_banks.tile([P, P], F32, name="columns_ps", tag="flip")
+        nc.tensor.transpose(columns_ps[:], rows[:], ident_f32[:])
+        columns = held.tile([P, ROWS_USED], F32, name="columns")
+        nc.vector.tensor_copy(columns[:], columns_ps[:, 0:ROWS_USED])
+
+        def column(row):
+            return columns[:, row : row + 1]
+
+        res = [held.tile([P, N], F32, name=f"res{b}") for b in range(CHANNEL_BLOCKS)]
+        x = [held.tile([P, N], BF16, name=f"x{b}") for b in range(CHANNEL_BLOCKS)]
+        q = [held.tile([P, N], BF16, name=f"q{h}") for h in range(HEADS)]
+        k = [held.tile([P, N], BF16, name=f"k{h}") for h in range(HEADS)]
+        v_t = [held.tile([P, D], BF16, name=f"v_t{tb}") for tb in range(N // P)]
+        att = [held.tile([P, N], BF16, name=f"att{h}") for h in range(HEADS)]
+
+        def embed_and_norm(c):
+            chunk = slice(c * CHUNK, (c + 1) * CHUNK)
+            piece = offsets[:, c * CHUNK // 16 : (c + 1) * CHUNK // 16]
+            for b in range(CHANNEL_BLOCKS):
+                nc.vector.tensor_tensor(
+                    res[b][:, chunk], table[b][:].indirect(piece), pos_sb[b][:, chunk], ALU.add
+                )
+            mean_var = small.tile([P, BLOCKS_PER_CHUNK, 2], F32, name="mean_var")
+            res_t = []
+            for u in range(BLOCKS_PER_CHUNK):
+                flipped = token_banks.tile([P, D], F32, name="res_t", tag="bank")
+                for b in range(CHANNEL_BLOCKS):
+                    nc.tensor.transpose(
+                        flipped[:, block(b)], res[b][:, block(c * BLOCKS_PER_CHUNK + u)], ident_f32[:]
+                    )
+                stats = small.tile([P, 6], F32, name="stats")
+                nc.vector.bn_stats(stats[:], flipped[:])
+                nc.vector.bn_aggr(mean_var[:, u, :], stats[:])
+                res_t.append(flipped)
+            sd = small.tile([P, BLOCKS_PER_CHUNK, 1], F32, name="sd")
+            nc.scalar.activation(sd[:], mean_var[:, :, 1:2], FUNC.Sqrt)
+            sd_eps = small.tile([P, BLOCKS_PER_CHUNK, 1], F32, name="sd_eps")
+            nc.vector.tensor_scalar_add(sd_eps[:], sd[:], EPS)
+            inv_sd = small.tile([P, BLOCKS_PER_CHUNK, 1], F32, name="inv_sd")
+            nc.vector.reciprocal(inv_sd[:], sd_eps[:])
+            normed_t = []
+            for u in range(BLOCKS_PER_CHUNK):
+                normed = work.tile([P, D], F32, name="normed_t", bufs=BLOCKS_PER_CHUNK)
+                nc.vector.tensor_scalar(
+                    normed[:], res_t[u][:], mean_var[:, u, 0:1], inv_sd[:, u, :], ALU.subtract, ALU.mult
+                )
+                normed_t.append(normed)
+            for b in range(CHANNEL_BLOCKS):
+                normed_ps = flip_banks.tile([P, CHUNK], F32, name="normed_ps", tag="flip")
+                for u in range(BLOCKS_PER_CHUNK):
+                    nc.tensor.transpose(normed_ps[:, block(u)], normed_t[u][:, block(b)], ident_f32[:])
+                nc.scalar.activation(
+                    x[b][:, chunk],
+                    normed_ps[:],
+                    FUNC.Identity,
+                    bias=column(ROW_LN_B + b),
+                    scale=column(ROW_LN_W + b),
+                )
+
+        def project_qk(c, h):
+            chunk = slice(c * CHUNK, (c + 1) * CHUNK)
+            for dest, m in ((q[h], h), (k[h], HEADS + h)):
+                product = product_banks.tile([P, CHUNK], F32, name="qk_ps", tag="product")
+                for b in range(CHANNEL_BLOCKS):
+                    nc.tensor.matmul(
+                        product[:],
+                        w_attn_sb[b][:, block(m)],
+                        x[b][:, chunk],
+                        start=(b == 0),
+                        stop=(b == CHANNEL_BLOCKS - 1),
+                    )
+                nc.scalar.activation(
+                    dest[:, chunk], product[:], FUNC.Identity, bias=column(ROW_B_QK + m)
+                )
+
+        def project_v(c):
+            for tb in range(c * BLOCKS_PER_CHUNK, (c + 1) * BLOCKS_PER_CHUNK):
+                product = product_banks.tile([P, D], F32, name="v_ps", tag="product")
+                for b in range(CHANNEL_BLOCKS):
+                    nc.tensor.matmul(
+                        product[:],
+                        x[b][:, block(tb)],
+                        w_attn_sb[b][:, 2 * D : 3 * D],
+                        start=(b == 0),
+                        stop=(b == CHANNEL_BLOCKS - 1),
+                    )
+                nc.vector.tensor_tensor(v_t[tb][:], product[:], b_v_all[:], ALU.add)
+
+        def attend(c, h):
+            chunk = slice(c * CHUNK, (c + 1) * CHUNK)
+            key_blocks = (c + 1) * BLOCKS_PER_CHUNK
+            n_banks = c + 1
+            exp_t = work.tile([P, key_blocks, CHUNK], BF16, name="exp_t")
+            exp_sums = small.tile([P, BLOCKS_PER_CHUNK, n_banks], F32, name="exp_sums")
+            for u in range(BLOCKS_PER_CHUNK):
+                jb = c * BLOCKS_PER_CHUNK + u
+                keys = (jb + 1) * P
+                widths = [min(CHUNK, keys - i * CHUNK) for i in range(n_banks)]
+                scores = []
+                for i, width in enumerate(widths):
+                    bank = token_banks.tile([P, CHUNK], F32, name="scores", tag="bank")
+                    diagonal = i == n_banks - 1
+                    nc.tensor.matmul(
+                        bank[:, 0:width],
+                        q[h][:, block(jb)],
+                        k[h][:, i * CHUNK : i * CHUNK + width],
+                        start=True,
+                        stop=not diagonal,
+                    )
+                    if diagonal:
+                        nc.tensor.matmul(
+                            bank[:, width - P : width], ident_bf16[:], causal[:], start=False, stop=True
+                        )
+                    scores.append(bank)
+                neg_max = small.tile([P, n_banks], F32, name="neg_max")
+                for i, width in enumerate(widths):
+                    nc.vector.tensor_reduce(
+                        neg_max[:, i : i + 1], scores[i][:, 0:width], axis=AXIS.X, op=ALU.max, negate=True
+                    )
+                bias = small.tile([P, 1], F32, name="bias")
+                nc.vector.tensor_scalar(
+                    bias[:], neg_max[:, 0:1], neg_max[:, n_banks - 1 : n_banks], SCORE_SCALE, ALU.min, ALU.mult
+                )
+                exps = work.tile([P, N], BF16, name="exps", bufs=3)
+                for i, width in enumerate(widths):
+                    nc.scalar.activation(
+                        exps[:, i * CHUNK : i * CHUNK + width],
+                        scores[i][:, 0:width],
+                        FUNC.Exp,
+                        bias=bias[:],
+                        scale=SCORE_SCALE,
+                        accum_out=exp_sums[:, u, i : i + 1],
+                    )
+                flipped = flip_banks.tile([P, N], BF16, name="exps_ps", tag="flip")
+                for tb in range(jb + 1):
+                    nc.tensor.transpose(flipped[:, block(tb)], exps[:, block(tb)], ident_bf16[:])
+                nc.scalar.copy(
+                    exp_t[:, 0 : jb + 1, block(u)],
+                    flipped[:, 0:keys].rearrange("p (tb j) -> p tb j", j=P),
+                )
+            weighted = product_banks.tile([P, CHUNK], F32, name="weighted", tag="product")
+            for tb in range(key_blocks):
+                first = max(0, tb - c * BLOCKS_PER_CHUNK) * P
+                nc.tensor.matmul(
+                    weighted[:, first:CHUNK],
+                    v_t[tb][:, block(h)],
+                    exp_t[:, tb, first:CHUNK],
+                    start=(tb == 0),
+                    stop=(tb == key_blocks - 1),
+                )
+            total = small.tile([P, BLOCKS_PER_CHUNK], F32, name="total")
+            nc.vector.tensor_reduce(total[:], exp_sums[:], axis=AXIS.X, op=ALU.add)
+            inv_total = small.tile([P, BLOCKS_PER_CHUNK], F32, name="inv_total")
+            nc.vector.reciprocal(inv_total[:], total[:])
+            repeated = work.tile([P, BLOCKS_PER_CHUNK, P], F32, name="repeated")
+            nc.gpsimd.tensor_copy(
+                repeated[:], inv_total[:].unsqueeze(2).to_broadcast([P, BLOCKS_PER_CHUNK, P])
+            )
+            inv_ps = flip_banks.tile([P, CHUNK], F32, name="inv_ps", tag="flip")
+            for u in range(BLOCKS_PER_CHUNK):
+                nc.tensor.transpose(inv_ps[:, block(u)], repeated[:, u, :], ident_f32[:])
+            inv_rows = work.tile([P, CHUNK], F32, name="inv_rows")
+            nc.scalar.copy(inv_rows[:], inv_ps[:])
+            nc.vector.tensor_tensor(att[h][:, chunk], weighted[:], inv_rows[:], ALU.mult)
+
+        def project_out(c):
+            chunk = slice(c * CHUNK, (c + 1) * CHUNK)
+            for m in range(CHANNEL_BLOCKS):
+                product = product_banks.tile([P, CHUNK], F32, name="out_ps", tag="product")
+                for h in range(HEADS):
+                    nc.tensor.matmul(
+                        product[:],
+                        w_o_sb[h][:, block(m)],
+                        att[h][:, chunk],
+                        start=(h == 0),
+                        stop=(h == HEADS - 1),
+                    )
+                out_sb = work.tile([P, CHUNK], F32, name="out_sb", bufs=3)
+                nc.vector.scalar_tensor_tensor(
+                    out_sb[:], product[:], column(ROW_B_O + m), res[m][:, chunk], ALU.add, ALU.add
+                )
+                nc.sync.dma_start(out[block(m), chunk], out_sb[:])
+
+        for c in range(CHUNKS):
+            embed_and_norm(c)
+        for c in range(CHUNKS):
+            for h in range(HEADS):
+                project_qk(c, h)
+                if h == 0:
+                    project_v(c)
+                attend(c, h)
+            project_out(c)

@@ -179,82 +179,105 @@ def tile_jtransformer_b_kernel(
                     )
                 nc.vector.tensor_tensor(v_t[tb][:], product[:], b_v_all[:], ALU.add)
 
-        def attend(c, h):
-            chunk = slice(c * CHUNK, (c + 1) * CHUNK)
-            key_blocks = (c + 1) * BLOCKS_PER_CHUNK
+        groups = [(c, h) for c in range(CHUNKS) for h in range(HEADS)]
+        exp_t = {}
+        exp_sums = {}
+        exps = {}
+        inv_rows = {}
+        weighted = {}
+
+        def exponentials(g, u):
+            c, h = groups[g]
             n_banks = c + 1
-            exp_t = work.tile([P, key_blocks, CHUNK], BF16, name="exp_t")
-            exp_sums = small.tile([P, BLOCKS_PER_CHUNK, n_banks], F32, name="exp_sums")
-            for u in range(BLOCKS_PER_CHUNK):
-                jb = c * BLOCKS_PER_CHUNK + u
-                keys = (jb + 1) * P
-                widths = [min(CHUNK, keys - i * CHUNK) for i in range(n_banks)]
-                scores = []
-                for i, width in enumerate(widths):
-                    bank = token_banks.tile([P, CHUNK], F32, name="scores", tag="bank")
-                    diagonal = i == n_banks - 1
-                    nc.tensor.matmul(
-                        bank[:, 0:width],
-                        q[h][:, block(jb)],
-                        k[h][:, i * CHUNK : i * CHUNK + width],
-                        start=True,
-                        stop=not diagonal,
-                    )
-                    if diagonal:
-                        nc.tensor.matmul(
-                            bank[:, width - P : width], ident_bf16[:], causal[:], start=False, stop=True
-                        )
-                    scores.append(bank)
-                neg_max = small.tile([P, n_banks], F32, name="neg_max")
-                for i, width in enumerate(widths):
-                    nc.vector.tensor_reduce(
-                        neg_max[:, i : i + 1], scores[i][:, 0:width], axis=AXIS.X, op=ALU.max, negate=True
-                    )
-                bias = small.tile([P, 1], F32, name="bias")
-                nc.vector.tensor_scalar(
-                    bias[:], neg_max[:, 0:1], neg_max[:, n_banks - 1 : n_banks], SCORE_SCALE, ALU.min, ALU.mult
-                )
-                exps = work.tile([P, N], BF16, name="exps", bufs=3)
-                for i, width in enumerate(widths):
-                    nc.scalar.activation(
-                        exps[:, i * CHUNK : i * CHUNK + width],
-                        scores[i][:, 0:width],
-                        FUNC.Exp,
-                        bias=bias[:],
-                        scale=SCORE_SCALE,
-                        accum_out=exp_sums[:, u, i : i + 1],
-                    )
-                flipped = flip_banks.tile([P, N], BF16, name="exps_ps", tag="flip")
-                for tb in range(jb + 1):
-                    nc.tensor.transpose(flipped[:, block(tb)], exps[:, block(tb)], ident_bf16[:])
-                nc.scalar.copy(
-                    exp_t[:, 0 : jb + 1, block(u)],
-                    flipped[:, 0:keys].rearrange("p (tb j) -> p tb j", j=P),
-                )
-            weighted = product_banks.tile([P, CHUNK], F32, name="weighted", tag="product")
-            for tb in range(key_blocks):
-                first = max(0, tb - c * BLOCKS_PER_CHUNK) * P
+            if u == 0:
+                exp_sums[g] = small.tile([P, BLOCKS_PER_CHUNK, n_banks], F32, name="exp_sums")
+            jb = c * BLOCKS_PER_CHUNK + u
+            keys = (jb + 1) * P
+            widths = [min(CHUNK, keys - i * CHUNK) for i in range(n_banks)]
+            scores = []
+            for i, width in enumerate(widths):
+                bank = token_banks.tile([P, CHUNK], F32, name="scores", tag="bank")
+                diagonal = i == n_banks - 1
                 nc.tensor.matmul(
-                    weighted[:, first:CHUNK],
-                    v_t[tb][:, block(h)],
-                    exp_t[:, tb, first:CHUNK],
-                    start=(tb == 0),
-                    stop=(tb == key_blocks - 1),
+                    bank[:, 0:width],
+                    q[h][:, block(jb)],
+                    k[h][:, i * CHUNK : i * CHUNK + width],
+                    start=True,
+                    stop=not diagonal,
                 )
+                if diagonal:
+                    nc.tensor.matmul(
+                        bank[:, width - P : width], ident_bf16[:], causal[:], start=False, stop=True
+                    )
+                scores.append(bank)
+            neg_max = small.tile([P, n_banks], F32, name="neg_max")
+            for i, width in enumerate(widths):
+                nc.vector.tensor_reduce(
+                    neg_max[:, i : i + 1], scores[i][:, 0:width], axis=AXIS.X, op=ALU.max, negate=True
+                )
+            bias = small.tile([P, 1], F32, name="bias")
+            nc.vector.tensor_scalar(
+                bias[:], neg_max[:, 0:1], neg_max[:, n_banks - 1 : n_banks], SCORE_SCALE, ALU.min, ALU.mult
+            )
+            exps[g, u] = work.tile([P, N], BF16, name="exps", bufs=4)
+            for i, width in enumerate(widths):
+                nc.scalar.activation(
+                    exps[g, u][:, i * CHUNK : i * CHUNK + width],
+                    scores[i][:, 0:width],
+                    FUNC.Exp,
+                    bias=bias[:],
+                    scale=SCORE_SCALE,
+                    accum_out=exp_sums[g][:, u, i : i + 1],
+                )
+
+        def flip(g, u):
+            c, h = groups[g]
+            if u == 0:
+                exp_t[g] = work.tile([P, (c + 1) * BLOCKS_PER_CHUNK, CHUNK], BF16, name="exp_t")
+            jb = c * BLOCKS_PER_CHUNK + u
+            flipped = flip_banks.tile([P, N], BF16, name="exps_ps", tag="flip")
+            for tb in range(jb + 1):
+                nc.tensor.transpose(flipped[:, block(tb)], exps[g, u][:, block(tb)], ident_bf16[:])
+            nc.scalar.copy(
+                exp_t[g][:, 0 : jb + 1, block(u)],
+                flipped[:, 0 : (jb + 1) * P].rearrange("p (tb j) -> p tb j", j=P),
+            )
+
+        def invert_sums(g):
             total = small.tile([P, BLOCKS_PER_CHUNK], F32, name="total")
-            nc.vector.tensor_reduce(total[:], exp_sums[:], axis=AXIS.X, op=ALU.add)
+            nc.vector.tensor_reduce(total[:], exp_sums[g][:], axis=AXIS.X, op=ALU.add)
             inv_total = small.tile([P, BLOCKS_PER_CHUNK], F32, name="inv_total")
             nc.vector.reciprocal(inv_total[:], total[:])
             repeated = work.tile([P, BLOCKS_PER_CHUNK, P], F32, name="repeated")
             nc.gpsimd.tensor_copy(
                 repeated[:], inv_total[:].unsqueeze(2).to_broadcast([P, BLOCKS_PER_CHUNK, P])
             )
+            return repeated
+
+        def weighted_sum(g, repeated):
+            c, h = groups[g]
             inv_ps = flip_banks.tile([P, CHUNK], F32, name="inv_ps", tag="flip")
             for u in range(BLOCKS_PER_CHUNK):
                 nc.tensor.transpose(inv_ps[:, block(u)], repeated[:, u, :], ident_f32[:])
-            inv_rows = work.tile([P, CHUNK], F32, name="inv_rows")
-            nc.scalar.copy(inv_rows[:], inv_ps[:])
-            nc.vector.tensor_tensor(att[h][:, chunk], weighted[:], inv_rows[:], ALU.mult)
+            inv_rows[g] = work.tile([P, CHUNK], F32, name="inv_rows")
+            nc.scalar.copy(inv_rows[g][:], inv_ps[:])
+            key_blocks = (c + 1) * BLOCKS_PER_CHUNK
+            weighted[g] = product_banks.tile([P, CHUNK], F32, name="weighted", tag="product")
+            for tb in range(key_blocks):
+                first = max(0, tb - c * BLOCKS_PER_CHUNK) * P
+                nc.tensor.matmul(
+                    weighted[g][:, first:CHUNK],
+                    v_t[tb][:, block(h)],
+                    exp_t[g][:, tb, first:CHUNK],
+                    start=(tb == 0),
+                    stop=(tb == key_blocks - 1),
+                )
+
+        def divide(g):
+            c, h = groups[g]
+            nc.vector.tensor_tensor(
+                att[h][:, c * CHUNK : (c + 1) * CHUNK], weighted[g][:], inv_rows[g][:], ALU.mult
+            )
 
         def project_out(c):
             chunk = slice(c * CHUNK, (c + 1) * CHUNK)
@@ -276,10 +299,32 @@ def tile_jtransformer_b_kernel(
 
         for c in range(CHUNKS):
             embed_and_norm(c)
-        for c in range(CHUNKS):
-            for h in range(HEADS):
-                project_qk(c, h)
-                if h == 0:
-                    project_v(c)
-                attend(c, h)
-            project_out(c)
+        project_qk(0, 0)
+        project_v(0)
+
+        n_units = len(groups) * BLOCKS_PER_CHUNK
+
+        def group_ended(s):
+            if 0 <= s < n_units and s % BLOCKS_PER_CHUNK == BLOCKS_PER_CHUNK - 1:
+                return s // BLOCKS_PER_CHUNK
+            return None
+
+        repeated = {}
+        for s in range(n_units + 6):
+            if s < n_units:
+                g, u = divmod(s, BLOCKS_PER_CHUNK)
+                exponentials(g, u)
+                if u == 0 and g + 1 < len(groups):
+                    project_qk(*groups[g + 1])
+                    if groups[g + 1][1] == 0:
+                        project_v(groups[g + 1][0])
+            if group_ended(s - 1) is not None:
+                repeated[group_ended(s - 1)] = invert_sums(group_ended(s - 1))
+            if 0 <= s - 2 < n_units:
+                flip(*divmod(s - 2, BLOCKS_PER_CHUNK))
+            if group_ended(s - 3) is not None:
+                weighted_sum(group_ended(s - 3), repeated[group_ended(s - 3)])
+            if group_ended(s - 4) is not None:
+                divide(group_ended(s - 4))
+            if group_ended(s - 5) is not None and groups[group_ended(s - 5)][1] == HEADS - 1:
+                project_out(groups[group_ended(s - 5)][0])

@@ -10,7 +10,6 @@ U16 = mybir.dt.uint16
 I32 = mybir.dt.int32
 ALU = mybir.AluOpType
 FUNC = mybir.ActivationFunctionType
-AXIS = mybir.AxisListType
 
 P = 128
 D = 512
@@ -190,11 +189,12 @@ def tile_jtransformer_b_kernel(
             c, h = groups[g]
             n_banks = c + 1
             if u == 0:
-                exp_sums[g] = small.tile([P, BLOCKS_PER_CHUNK, n_banks], F32, name="exp_sums")
+                exp_sums[g] = small.tile([P, BLOCKS_PER_CHUNK], F32, name="exp_sums")
             jb = c * BLOCKS_PER_CHUNK + u
             keys = (jb + 1) * P
             widths = [min(CHUNK, keys - i * CHUNK) for i in range(n_banks)]
-            scores = []
+            neg_scores = work.tile([P, N], F32, name="neg_scores", bufs=3)
+            neg_max = small.tile([P, n_banks], F32, name="neg_max")
             for i, width in enumerate(widths):
                 bank = token_banks.tile([P, CHUNK], F32, name="scores", tag="bank")
                 diagonal = i == n_banks - 1
@@ -209,26 +209,24 @@ def tile_jtransformer_b_kernel(
                     nc.tensor.matmul(
                         bank[:, width - P : width], ident_bf16[:], causal[:], start=False, stop=True
                     )
-                scores.append(bank)
-            neg_max = small.tile([P, n_banks], F32, name="neg_max")
-            for i, width in enumerate(widths):
-                nc.vector.tensor_reduce(
-                    neg_max[:, i : i + 1], scores[i][:, 0:width], axis=AXIS.X, op=ALU.max, negate=True
+                nc.vector.tensor_scalar(
+                    neg_scores[:, i * CHUNK : i * CHUNK + width],
+                    bank[:, 0:width],
+                    -SCORE_SCALE,
+                    None if i == 0 else neg_max[:, i - 1 : i],
+                    ALU.mult,
+                    ALU.min,
+                    accum_out=neg_max[:, i : i + 1],
                 )
-            bias = small.tile([P, 1], F32, name="bias")
-            nc.vector.tensor_scalar(
-                bias[:], neg_max[:, 0:1], neg_max[:, n_banks - 1 : n_banks], SCORE_SCALE, ALU.min, ALU.mult
-            )
             exps[g, u] = work.tile([P, N], BF16, name="exps", bufs=4)
-            for i, width in enumerate(widths):
-                nc.scalar.activation(
-                    exps[g, u][:, i * CHUNK : i * CHUNK + width],
-                    scores[i][:, 0:width],
-                    FUNC.Exp,
-                    bias=bias[:],
-                    scale=SCORE_SCALE,
-                    accum_out=exp_sums[g][:, u, i : i + 1],
-                )
+            nc.scalar.activation(
+                exps[g, u][:, 0:keys],
+                neg_scores[:, 0:keys],
+                FUNC.Exp,
+                bias=neg_max[:, n_banks - 1 : n_banks],
+                scale=-1.0,
+                accum_out=exp_sums[g][:, u : u + 1],
+            )
 
         def flip(g, u):
             c, h = groups[g]
@@ -238,16 +236,14 @@ def tile_jtransformer_b_kernel(
             flipped = flip_banks.tile([P, N], BF16, name="exps_ps", tag="flip")
             for tb in range(jb + 1):
                 nc.tensor.transpose(flipped[:, block(tb)], exps[g, u][:, block(tb)], ident_bf16[:])
-            nc.scalar.copy(
+            nc.vector.tensor_copy(
                 exp_t[g][:, 0 : jb + 1, block(u)],
                 flipped[:, 0 : (jb + 1) * P].rearrange("p (tb j) -> p tb j", j=P),
             )
 
         def invert_sums(g):
-            total = small.tile([P, BLOCKS_PER_CHUNK], F32, name="total")
-            nc.vector.tensor_reduce(total[:], exp_sums[g][:], axis=AXIS.X, op=ALU.add)
             inv_total = small.tile([P, BLOCKS_PER_CHUNK], F32, name="inv_total")
-            nc.vector.reciprocal(inv_total[:], total[:])
+            nc.vector.reciprocal(inv_total[:], exp_sums[g][:])
             repeated = work.tile([P, BLOCKS_PER_CHUNK, P], F32, name="repeated")
             nc.gpsimd.tensor_copy(
                 repeated[:], inv_total[:].unsqueeze(2).to_broadcast([P, BLOCKS_PER_CHUNK, P])

@@ -68,8 +68,6 @@ def tile_jtransformer_b_kernel(
         for b in range(CHANNEL_BLOCKS):
             nc.sync.dma_start(table[b][:], embed[block(b), :])
             nc.sync.dma_start(pos_sb[b][:, 0:CHUNK], pos[block(b), 0:CHUNK])
-        for b in range(CHANNEL_BLOCKS):
-            nc.sync.dma_start(pos_sb[b][:, CHUNK:N], pos[block(b), CHUNK:N])
         w_attn_sb = [held.tile([P, 3 * D], BF16, name=f"w_attn_sb{b}") for b in range(CHANNEL_BLOCKS)]
         for b in range(CHANNEL_BLOCKS):
             nc.sync.dma_start(w_attn_sb[b][:], w_attn[block(b), :])
@@ -77,6 +75,8 @@ def tile_jtransformer_b_kernel(
         nc.sync.dma_start(
             b_v_all[:], b_attn[2 * D : 3 * D, :].rearrange("e o -> (e o)").partition_broadcast(P)
         )
+        for b in range(CHANNEL_BLOCKS):
+            nc.sync.dma_start(pos_sb[b][:, CHUNK:N], pos[block(b), CHUNK:N])
         w_o_sb = [held.tile([P, D], BF16, name=f"w_o_sb{b}") for b in range(CHANNEL_BLOCKS)]
         for b in range(CHANNEL_BLOCKS):
             nc.sync.dma_start(w_o_sb[b][:], w_o[block(b), :])
@@ -89,6 +89,11 @@ def tile_jtransformer_b_kernel(
         nc.gpsimd.iota(key_minus_query[:], pattern=[[1, P]], base=0, channel_multiplier=-1)
         causal = held.tile([P, P], BF16, name="causal")
         nc.vector.tensor_scalar(causal[:], key_minus_query[:], 0.0, MASKED, ALU.is_gt, ALU.mult)
+
+        half = held.tile([P, 1], F32, name="half")
+        nc.gpsimd.memset(half[:], 0.5)
+        warmed = held.tile([P, 1], F32, name="warmed")
+        nc.scalar.activation(warmed[:], half[:], FUNC.Exp)
 
         columns_ps = flip_banks.tile([P, P], F32, name="columns_ps", tag="flip")
         nc.tensor.transpose(columns_ps[:], rows[:], ident_f32[:])
@@ -105,49 +110,71 @@ def tile_jtransformer_b_kernel(
         v_t = [held.tile([P, D], BF16, name=f"v_t{tb}") for tb in range(N // P)]
         att = [held.tile([P, N], BF16, name=f"att{h}") for h in range(HEADS)]
 
-        def embed_and_norm(c):
+        def look_up(c, b):
             chunk = slice(c * CHUNK, (c + 1) * CHUNK)
             piece = offsets[:, c * CHUNK // 16 : (c + 1) * CHUNK // 16]
+            nc.vector.tensor_tensor(
+                res[b][:, chunk], table[b][:].indirect(piece), pos_sb[b][:, chunk], ALU.add
+            )
+
+        res_t = {}
+        mean_var = {}
+        sd = {}
+        normed_t = {}
+
+        def moments(tb):
+            res_t[tb] = token_banks.tile([P, D], F32, name="res_t", tag="bank")
             for b in range(CHANNEL_BLOCKS):
-                nc.vector.tensor_tensor(
-                    res[b][:, chunk], table[b][:].indirect(piece), pos_sb[b][:, chunk], ALU.add
-                )
-            mean_var = small.tile([P, BLOCKS_PER_CHUNK, 2], F32, name="mean_var")
-            res_t = []
-            for u in range(BLOCKS_PER_CHUNK):
-                flipped = token_banks.tile([P, D], F32, name="res_t", tag="bank")
-                for b in range(CHANNEL_BLOCKS):
-                    nc.tensor.transpose(
-                        flipped[:, block(b)], res[b][:, block(c * BLOCKS_PER_CHUNK + u)], ident_f32[:]
-                    )
-                stats = small.tile([P, 6], F32, name="stats")
-                nc.vector.bn_stats(stats[:], flipped[:])
-                nc.vector.bn_aggr(mean_var[:, u, :], stats[:])
-                res_t.append(flipped)
-            sd = small.tile([P, BLOCKS_PER_CHUNK, 1], F32, name="sd")
-            nc.scalar.activation(sd[:], mean_var[:, :, 1:2], FUNC.Sqrt)
-            sd_eps = small.tile([P, BLOCKS_PER_CHUNK, 1], F32, name="sd_eps")
-            nc.vector.tensor_scalar_add(sd_eps[:], sd[:], EPS)
-            inv_sd = small.tile([P, BLOCKS_PER_CHUNK, 1], F32, name="inv_sd")
+                nc.tensor.transpose(res_t[tb][:, block(b)], res[b][:, block(tb)], ident_f32[:])
+            stats = small.tile([P, 6], F32, name="stats")
+            nc.vector.bn_stats(stats[:], res_t[tb][:])
+            mean_var[tb] = small.tile([P, 2], F32, name="mean_var")
+            nc.vector.bn_aggr(mean_var[tb][:], stats[:])
+            sd[tb] = small.tile([P, 1], F32, name="sd")
+            nc.gpsimd.tensor_tensor(sd[tb][:], mean_var[tb][:, 1:2], half[:], ALU.pow)
+
+        def normalise(tb):
+            sd_eps = small.tile([P, 1], F32, name="sd_eps")
+            nc.vector.tensor_scalar_add(sd_eps[:], sd[tb][:], EPS)
+            inv_sd = small.tile([P, 1], F32, name="inv_sd")
             nc.vector.reciprocal(inv_sd[:], sd_eps[:])
-            normed_t = []
-            for u in range(BLOCKS_PER_CHUNK):
-                normed = work.tile([P, D], F32, name="normed_t", bufs=BLOCKS_PER_CHUNK)
-                nc.vector.tensor_scalar(
-                    normed[:], res_t[u][:], mean_var[:, u, 0:1], inv_sd[:, u, :], ALU.subtract, ALU.mult
-                )
-                normed_t.append(normed)
+            normed_t[tb] = work.tile([P, D], F32, name="normed_t", bufs=3)
+            nc.vector.tensor_scalar(
+                normed_t[tb][:], res_t[tb][:], mean_var[tb][:, 0:1], inv_sd[:], ALU.subtract, ALU.mult
+            )
+
+        def flip_back(tb):
+            normed_ps = flip_banks.tile([P, CHANNEL_BLOCKS, P], F32, name="normed_ps", tag="flip")
             for b in range(CHANNEL_BLOCKS):
-                normed_ps = flip_banks.tile([P, CHUNK], F32, name="normed_ps", tag="flip")
-                for u in range(BLOCKS_PER_CHUNK):
-                    nc.tensor.transpose(normed_ps[:, block(u)], normed_t[u][:, block(b)], ident_f32[:])
+                nc.tensor.transpose(normed_ps[:, b, :], normed_t[tb][:, block(b)], ident_f32[:])
+            for b in range(CHANNEL_BLOCKS):
                 nc.scalar.activation(
-                    x[b][:, chunk],
-                    normed_ps[:],
+                    x[b][:, block(tb)],
+                    normed_ps[:, b, :],
                     FUNC.Identity,
                     bias=column(ROW_LN_B + b),
                     scale=column(ROW_LN_W + b),
                 )
+
+        def project_v(tb):
+            product = product_banks.tile([P, D], F32, name="v_ps", tag="product")
+            for b in range(CHANNEL_BLOCKS):
+                nc.tensor.matmul(
+                    product[:],
+                    x[b][:, block(tb)],
+                    w_attn_sb[b][:, 2 * D : 3 * D],
+                    start=(b == 0),
+                    stop=(b == CHANNEL_BLOCKS - 1),
+                )
+            nc.vector.tensor_tensor(v_t[tb][:], product[:], b_v_all[:], ALU.add)
+
+        PREPARE_STEPS = BLOCKS_PER_CHUNK + 3
+
+        def prepare(c, i):
+            first = c * BLOCKS_PER_CHUNK
+            for behind, stage in enumerate((moments, normalise, flip_back, project_v)):
+                if 0 <= i - behind < BLOCKS_PER_CHUNK:
+                    stage(first + i - behind)
 
         def project_qk(c, h):
             chunk = slice(c * CHUNK, (c + 1) * CHUNK)
@@ -164,19 +191,6 @@ def tile_jtransformer_b_kernel(
                 nc.scalar.activation(
                     dest[:, chunk], product[:], FUNC.Identity, bias=column(ROW_B_QK + m)
                 )
-
-        def project_v(c):
-            for tb in range(c * BLOCKS_PER_CHUNK, (c + 1) * BLOCKS_PER_CHUNK):
-                product = product_banks.tile([P, D], F32, name="v_ps", tag="product")
-                for b in range(CHANNEL_BLOCKS):
-                    nc.tensor.matmul(
-                        product[:],
-                        x[b][:, block(tb)],
-                        w_attn_sb[b][:, 2 * D : 3 * D],
-                        start=(b == 0),
-                        stop=(b == CHANNEL_BLOCKS - 1),
-                    )
-                nc.vector.tensor_tensor(v_t[tb][:], product[:], b_v_all[:], ALU.add)
 
         groups = [(c, h) for c in range(CHUNKS) for h in range(HEADS)]
         exp_t = {}
@@ -275,28 +289,33 @@ def tile_jtransformer_b_kernel(
                 att[h][:, c * CHUNK : (c + 1) * CHUNK], weighted[g][:], inv_rows[g][:], ALU.mult
             )
 
-        def project_out(c):
+        out_ps = {}
+
+        def project_out(c, heads):
             chunk = slice(c * CHUNK, (c + 1) * CHUNK)
             for m in range(CHANNEL_BLOCKS):
-                product = product_banks.tile([P, CHUNK], F32, name="out_ps", tag="product")
-                for h in range(HEADS):
+                if heads[0] == 0:
+                    out_ps[c, m] = token_banks.tile([P, CHUNK], F32, name="out_ps", tag="bank")
+                for h in heads:
                     nc.tensor.matmul(
-                        product[:],
+                        out_ps[c, m][:],
                         w_o_sb[h][:, block(m)],
                         att[h][:, chunk],
                         start=(h == 0),
                         stop=(h == HEADS - 1),
                     )
-                out_sb = work.tile([P, CHUNK], F32, name="out_sb", bufs=3)
-                nc.vector.scalar_tensor_tensor(
-                    out_sb[:], product[:], column(ROW_B_O + m), res[m][:, chunk], ALU.add, ALU.add
-                )
-                nc.sync.dma_start(out[block(m), chunk], out_sb[:])
+                if heads[-1] == HEADS - 1:
+                    out_sb = work.tile([P, CHUNK], F32, name="out_sb", bufs=3)
+                    nc.vector.scalar_tensor_tensor(
+                        out_sb[:], out_ps[c, m][:], column(ROW_B_O + m), res[m][:, chunk], ALU.add, ALU.add
+                    )
+                    nc.sync.dma_start(out[block(m), chunk], out_sb[:])
 
-        for c in range(CHUNKS):
-            embed_and_norm(c)
+        for b in range(CHANNEL_BLOCKS):
+            look_up(0, b)
+        for i in range(PREPARE_STEPS):
+            prepare(0, i)
         project_qk(0, 0)
-        project_v(0)
 
         n_units = len(groups) * BLOCKS_PER_CHUNK
 
@@ -312,8 +331,6 @@ def tile_jtransformer_b_kernel(
                 exponentials(g, u)
                 if u == 0 and g + 1 < len(groups):
                     project_qk(*groups[g + 1])
-                    if groups[g + 1][1] == 0:
-                        project_v(groups[g + 1][0])
             if group_ended(s - 1) is not None:
                 repeated[group_ended(s - 1)] = invert_sums(group_ended(s - 1))
             if 0 <= s - 2 < n_units:
@@ -322,5 +339,15 @@ def tile_jtransformer_b_kernel(
                 weighted_sum(group_ended(s - 3), repeated[group_ended(s - 3)])
             if group_ended(s - 4) is not None:
                 divide(group_ended(s - 4))
-            if group_ended(s - 5) is not None and groups[group_ended(s - 5)][1] == HEADS - 1:
-                project_out(groups[group_ended(s - 5)][0])
+            if group_ended(s - 5) is not None:
+                c, h = groups[group_ended(s - 5)]
+                if c == CHUNKS - 1 and h == HEADS - 2:
+                    project_out(c, list(range(HEADS - 1)))
+                elif c == CHUNKS - 1 and h == HEADS - 1:
+                    project_out(c, [HEADS - 1])
+                elif h == HEADS - 1:
+                    project_out(c, list(range(HEADS)))
+            if s < CHANNEL_BLOCKS:
+                look_up(1, s)
+            elif s - CHANNEL_BLOCKS < PREPARE_STEPS:
+                prepare(1, s - CHANNEL_BLOCKS)

@@ -250,7 +250,7 @@ def tile_jtransformer_b_kernel(
             flipped = flip_banks.tile([P, N], BF16, name="exps_ps", tag="flip")
             for tb in range(jb + 1):
                 nc.tensor.transpose(flipped[:, block(tb)], exps[g, u][:, block(tb)], ident_bf16[:])
-            nc.vector.tensor_copy(
+            nc.scalar.copy(
                 exp_t[g][:, 0 : jb + 1, block(u)],
                 flipped[:, 0 : (jb + 1) * P].rearrange("p (tb j) -> p tb j", j=P),
             )

@@ -138,7 +138,7 @@ def tile_jtransformer_b_kernel(
             nc.vector.tensor_scalar_add(sd_eps[:], sd[tb][:], EPS)
             inv_sd = small.tile([P, 1], F32, name="inv_sd")
             nc.vector.reciprocal(inv_sd[:], sd_eps[:])
-            normed_t[tb] = work.tile([P, D], F32, name="normed_t", bufs=3)
+            normed_t[tb] = work.tile([P, D], F32, name="normed_t", bufs=4)
             nc.vector.tensor_scalar(
                 normed_t[tb][:], res_t[tb][:], mean_var[tb][:, 0:1], inv_sd[:], ALU.subtract, ALU.mult
             )
@@ -168,11 +168,11 @@ def tile_jtransformer_b_kernel(
                 )
             nc.vector.tensor_tensor(v_t[tb][:], product[:], b_v_all[:], ALU.add)
 
-        PREPARE_STEPS = BLOCKS_PER_CHUNK + 3
+        PREPARE_STEPS = BLOCKS_PER_CHUNK + 5
 
         def prepare(c, i):
             first = c * BLOCKS_PER_CHUNK
-            for behind, stage in enumerate((moments, normalise, flip_back, project_v)):
+            for behind, stage in ((0, moments), (1, normalise), (3, flip_back), (5, project_v)):
                 if 0 <= i - behind < BLOCKS_PER_CHUNK:
                     stage(first + i - behind)
 
@@ -232,7 +232,7 @@ def tile_jtransformer_b_kernel(
                     ALU.min,
                     accum_out=neg_max[:, i : i + 1],
                 )
-            exps[g, u] = work.tile([P, N], BF16, name="exps", bufs=4)
+            exps[g, u] = work.tile([P, N], BF16, name="exps", bufs=5)
             nc.scalar.activation(
                 exps[g, u][:, 0:keys],
                 neg_scores[:, 0:keys],
@@ -258,7 +258,7 @@ def tile_jtransformer_b_kernel(
         def invert_sums(g):
             inv_total = small.tile([P, BLOCKS_PER_CHUNK], F32, name="inv_total")
             nc.vector.reciprocal(inv_total[:], exp_sums[g][:])
-            repeated = work.tile([P, BLOCKS_PER_CHUNK, P], F32, name="repeated")
+            repeated = work.tile([P, BLOCKS_PER_CHUNK, P], F32, name="repeated", bufs=3)
             nc.gpsimd.tensor_copy(
                 repeated[:], inv_total[:].unsqueeze(2).to_broadcast([P, BLOCKS_PER_CHUNK, P])
             )
@@ -318,6 +318,7 @@ def tile_jtransformer_b_kernel(
         project_qk(0, 0)
 
         n_units = len(groups) * BLOCKS_PER_CHUNK
+        FLIP_LAG = 3
 
         def group_ended(s):
             if 0 <= s < n_units and s % BLOCKS_PER_CHUNK == BLOCKS_PER_CHUNK - 1:
@@ -325,22 +326,22 @@ def tile_jtransformer_b_kernel(
             return None
 
         repeated = {}
-        for s in range(n_units + 6):
+        for s in range(n_units + FLIP_LAG + 7):
             if s < n_units:
                 g, u = divmod(s, BLOCKS_PER_CHUNK)
                 exponentials(g, u)
                 if u == 0 and g + 1 < len(groups):
                     project_qk(*groups[g + 1])
-            if group_ended(s - 1) is not None:
-                repeated[group_ended(s - 1)] = invert_sums(group_ended(s - 1))
-            if 0 <= s - 2 < n_units:
-                flip(*divmod(s - 2, BLOCKS_PER_CHUNK))
-            if group_ended(s - 3) is not None:
-                weighted_sum(group_ended(s - 3), repeated[group_ended(s - 3)])
-            if group_ended(s - 4) is not None:
-                divide(group_ended(s - 4))
-            if group_ended(s - 5) is not None:
-                c, h = groups[group_ended(s - 5)]
+            if group_ended(s - 2) is not None:
+                repeated[group_ended(s - 2)] = invert_sums(group_ended(s - 2))
+            if 0 <= s - FLIP_LAG < n_units:
+                flip(*divmod(s - FLIP_LAG, BLOCKS_PER_CHUNK))
+            if group_ended(s - FLIP_LAG - 2) is not None:
+                weighted_sum(group_ended(s - FLIP_LAG - 2), repeated[group_ended(s - FLIP_LAG - 2)])
+            if group_ended(s - FLIP_LAG - 4) is not None:
+                divide(group_ended(s - FLIP_LAG - 4))
+            if group_ended(s - FLIP_LAG - 6) is not None:
+                c, h = groups[group_ended(s - FLIP_LAG - 6)]
                 if c == CHUNKS - 1 and h == HEADS - 2:
                     project_out(c, list(range(HEADS - 1)))
                 elif c == CHUNKS - 1 and h == HEADS - 1:

@@ -67,14 +67,18 @@ def tile_jtransformer_b_kernel(
         pos_sb = [held.tile([P, N], F32, name=f"pos_sb{b}") for b in range(CHANNEL_BLOCKS)]
         for b in range(CHANNEL_BLOCKS):
             nc.sync.dma_start(table[b][:], embed[block(b), :])
-            nc.sync.dma_start(pos_sb[b][:, 0:CHUNK], pos[block(b), 0:CHUNK])
+            nc.sync.dma_start(pos_sb[b][:, 0:P], pos[block(b), 0:P])
+        for b in range(CHANNEL_BLOCKS):
+            nc.sync.dma_start(pos_sb[b][:, P:CHUNK], pos[block(b), P:CHUNK])
         w_attn_sb = [held.tile([P, 3 * D], BF16, name=f"w_attn_sb{b}") for b in range(CHANNEL_BLOCKS)]
         for b in range(CHANNEL_BLOCKS):
-            nc.sync.dma_start(w_attn_sb[b][:], w_attn[block(b), :])
+            nc.sync.dma_start(w_attn_sb[b][:, 2 * D : 3 * D], w_attn[block(b), 2 * D : 3 * D])
         b_v_all = held.tile([P, D], F32, name="b_v_all")
         nc.sync.dma_start(
             b_v_all[:], b_attn[2 * D : 3 * D, :].rearrange("e o -> (e o)").partition_broadcast(P)
         )
+        for b in range(CHANNEL_BLOCKS):
+            nc.sync.dma_start(w_attn_sb[b][:, 0 : 2 * D], w_attn[block(b), 0 : 2 * D])
         for b in range(CHANNEL_BLOCKS):
             nc.sync.dma_start(pos_sb[b][:, CHUNK:N], pos[block(b), CHUNK:N])
         w_o_sb = [held.tile([P, D], BF16, name=f"w_o_sb{b}") for b in range(CHANNEL_BLOCKS)]
@@ -110,11 +114,11 @@ def tile_jtransformer_b_kernel(
         v_t = [held.tile([P, D], BF16, name=f"v_t{tb}") for tb in range(N // P)]
         att = [held.tile([P, N], BF16, name=f"att{h}") for h in range(HEADS)]
 
-        def look_up(c, b):
-            chunk = slice(c * CHUNK, (c + 1) * CHUNK)
-            piece = offsets[:, c * CHUNK // 16 : (c + 1) * CHUNK // 16]
+        def look_up(b, first, count):
+            tokens = slice(first, first + count)
+            piece = offsets[:, first // 16 : (first + count) // 16]
             nc.vector.tensor_tensor(
-                res[b][:, chunk], table[b][:].indirect(piece), pos_sb[b][:, chunk], ALU.add
+                res[b][:, tokens], table[b][:].indirect(piece), pos_sb[b][:, tokens], ALU.add
             )
 
         res_t = {}
@@ -139,9 +143,18 @@ def tile_jtransformer_b_kernel(
             inv_sd = small.tile([P, 1], F32, name="inv_sd")
             nc.vector.reciprocal(inv_sd[:], sd_eps[:])
             normed_t[tb] = work.tile([P, D], F32, name="normed_t", bufs=4)
-            nc.vector.tensor_scalar(
-                normed_t[tb][:], res_t[tb][:], mean_var[tb][:, 0:1], inv_sd[:], ALU.subtract, ALU.mult
-            )
+            if tb < BLOCKS_PER_CHUNK:
+                minus_mean = small.tile([P, 1], F32, name="minus_mean")
+                nc.vector.tensor_scalar(
+                    minus_mean[:], mean_var[tb][:, 0:1], inv_sd[:], -1.0, ALU.mult, ALU.mult
+                )
+                nc.scalar.activation(
+                    normed_t[tb][:], res_t[tb][:], FUNC.Identity, bias=minus_mean[:], scale=inv_sd[:]
+                )
+            else:
+                nc.vector.tensor_scalar(
+                    normed_t[tb][:], res_t[tb][:], mean_var[tb][:, 0:1], inv_sd[:], ALU.subtract, ALU.mult
+                )
 
         def flip_back(tb):
             normed_ps = flip_banks.tile([P, CHANNEL_BLOCKS, P], F32, name="normed_ps", tag="flip")
@@ -305,16 +318,18 @@ def tile_jtransformer_b_kernel(
                         stop=(h == HEADS - 1),
                     )
                 if heads[-1] == HEADS - 1:
-                    out_sb = work.tile([P, CHUNK], F32, name="out_sb", bufs=3)
+                    out_sb = work.tile([P, CHUNK], F32, name="out_sb", bufs=CHANNEL_BLOCKS)
                     nc.vector.scalar_tensor_tensor(
                         out_sb[:], out_ps[c, m][:], column(ROW_B_O + m), res[m][:, chunk], ALU.add, ALU.add
                     )
                     nc.sync.dma_start(out[block(m), chunk], out_sb[:])
 
-        for b in range(CHANNEL_BLOCKS):
-            look_up(0, b)
-        for i in range(PREPARE_STEPS):
-            prepare(0, i)
+        for i in range(-1, PREPARE_STEPS):
+            if i + 1 < BLOCKS_PER_CHUNK:
+                for b in range(CHANNEL_BLOCKS):
+                    look_up(b, (i + 1) * P, P)
+            if i >= 0:
+                prepare(0, i)
         project_qk(0, 0)
 
         n_units = len(groups) * BLOCKS_PER_CHUNK
@@ -349,6 +364,6 @@ def tile_jtransformer_b_kernel(
                 elif h == HEADS - 1:
                     project_out(c, list(range(HEADS)))
             if s < CHANNEL_BLOCKS:
-                look_up(1, s)
+                look_up(s, CHUNK, CHUNK)
             elif s - CHANNEL_BLOCKS < PREPARE_STEPS:
                 prepare(1, s - CHANNEL_BLOCKS)

@@ -206,17 +206,15 @@ def tile_jtransformer_b_kernel(
                 )
 
         groups = [(c, h) for c in range(CHUNKS) for h in range(HEADS)]
-        exp_t = {}
-        exp_sums = {}
         exps = {}
-        inv_rows = {}
+        exp_sum = {}
+        probs = {}
+        probs_t = {}
         weighted = {}
 
         def exponentials(g, u):
             c, h = groups[g]
             n_banks = c + 1
-            if u == 0:
-                exp_sums[g] = small.tile([P, BLOCKS_PER_CHUNK], F32, name="exp_sums")
             jb = c * BLOCKS_PER_CHUNK + u
             keys = (jb + 1) * P
             widths = [min(CHUNK, keys - i * CHUNK) for i in range(n_banks)]
@@ -245,45 +243,42 @@ def tile_jtransformer_b_kernel(
                     ALU.min,
                     accum_out=neg_max[:, i : i + 1],
                 )
-            exps[g, u] = work.tile([P, N], BF16, name="exps", bufs=5)
+            exps[g, u] = work.tile([P, N], F32, name="exps", bufs=3)
+            exp_sum[g, u] = small.tile([P, 1], F32, name="exp_sum")
             nc.scalar.activation(
                 exps[g, u][:, 0:keys],
                 neg_scores[:, 0:keys],
                 FUNC.Exp,
                 bias=neg_max[:, n_banks - 1 : n_banks],
                 scale=-1.0,
-                accum_out=exp_sums[g][:, u : u + 1],
+                accum_out=exp_sum[g, u][:],
+            )
+
+        def divide(g, u):
+            c, h = groups[g]
+            keys = (c * BLOCKS_PER_CHUNK + u + 1) * P
+            inv_sum = small.tile([P, 1], F32, name="inv_sum")
+            nc.vector.reciprocal(inv_sum[:], exp_sum[g, u][:])
+            probs[g, u] = work.tile([P, N], BF16, name="probs", bufs=4)
+            nc.vector.tensor_scalar(
+                probs[g, u][:, 0:keys], exps[g, u][:, 0:keys], inv_sum[:], None, ALU.mult
             )
 
         def flip(g, u):
             c, h = groups[g]
             if u == 0:
-                exp_t[g] = work.tile([P, (c + 1) * BLOCKS_PER_CHUNK, CHUNK], BF16, name="exp_t")
+                probs_t[g] = work.tile([P, (c + 1) * BLOCKS_PER_CHUNK, CHUNK], BF16, name="probs_t")
             jb = c * BLOCKS_PER_CHUNK + u
-            flipped = flip_banks.tile([P, N], BF16, name="exps_ps", tag="flip")
+            flipped = flip_banks.tile([P, N], BF16, name="probs_ps", tag="flip")
             for tb in range(jb + 1):
-                nc.tensor.transpose(flipped[:, block(tb)], exps[g, u][:, block(tb)], ident_bf16[:])
+                nc.tensor.transpose(flipped[:, block(tb)], probs[g, u][:, block(tb)], ident_bf16[:])
             nc.scalar.copy(
-                exp_t[g][:, 0 : jb + 1, block(u)],
+                probs_t[g][:, 0 : jb + 1, block(u)],
                 flipped[:, 0 : (jb + 1) * P].rearrange("p (tb j) -> p tb j", j=P),
             )
 
-        def invert_sums(g):
-            inv_total = small.tile([P, BLOCKS_PER_CHUNK], F32, name="inv_total")
-            nc.vector.reciprocal(inv_total[:], exp_sums[g][:])
-            repeated = work.tile([P, BLOCKS_PER_CHUNK, P], F32, name="repeated", bufs=3)
-            nc.gpsimd.tensor_copy(
-                repeated[:], inv_total[:].unsqueeze(2).to_broadcast([P, BLOCKS_PER_CHUNK, P])
-            )
-            return repeated
-
-        def weighted_sum(g, repeated):
+        def weighted_sum(g):
             c, h = groups[g]
-            inv_ps = flip_banks.tile([P, CHUNK], F32, name="inv_ps", tag="flip")
-            for u in range(BLOCKS_PER_CHUNK):
-                nc.tensor.transpose(inv_ps[:, block(u)], repeated[:, u, :], ident_f32[:])
-            inv_rows[g] = work.tile([P, CHUNK], F32, name="inv_rows")
-            nc.scalar.copy(inv_rows[g][:], inv_ps[:])
             key_blocks = (c + 1) * BLOCKS_PER_CHUNK
             weighted[g] = product_banks.tile([P, CHUNK], F32, name="weighted", tag="product")
             for tb in range(key_blocks):
@@ -291,16 +286,14 @@ def tile_jtransformer_b_kernel(
                 nc.tensor.matmul(
                     weighted[g][:, first:CHUNK],
                     v_t[tb][:, block(h)],
-                    exp_t[g][:, tb, first:CHUNK],
+                    probs_t[g][:, tb, first:CHUNK],
                     start=(tb == 0),
                     stop=(tb == key_blocks - 1),
                 )
 
-        def divide(g):
+        def round_att(g):
             c, h = groups[g]
-            nc.vector.tensor_tensor(
-                att[h][:, c * CHUNK : (c + 1) * CHUNK], weighted[g][:], inv_rows[g][:], ALU.mult
-            )
+            nc.scalar.copy(att[h][:, c * CHUNK : (c + 1) * CHUNK], weighted[g][:])
 
         out_ps = {}
 
@@ -340,21 +333,20 @@ def tile_jtransformer_b_kernel(
                 return s // BLOCKS_PER_CHUNK
             return None
 
-        repeated = {}
         for s in range(n_units + FLIP_LAG + 7):
             if s < n_units:
                 g, u = divmod(s, BLOCKS_PER_CHUNK)
                 exponentials(g, u)
                 if u == 0 and g + 1 < len(groups):
                     project_qk(*groups[g + 1])
-            if group_ended(s - 2) is not None:
-                repeated[group_ended(s - 2)] = invert_sums(group_ended(s - 2))
+            if 0 <= s - 1 < n_units:
+                divide(*divmod(s - 1, BLOCKS_PER_CHUNK))
             if 0 <= s - FLIP_LAG < n_units:
                 flip(*divmod(s - FLIP_LAG, BLOCKS_PER_CHUNK))
             if group_ended(s - FLIP_LAG - 2) is not None:
-                weighted_sum(group_ended(s - FLIP_LAG - 2), repeated[group_ended(s - FLIP_LAG - 2)])
+                weighted_sum(group_ended(s - FLIP_LAG - 2))
             if group_ended(s - FLIP_LAG - 4) is not None:
-                divide(group_ended(s - FLIP_LAG - 4))
+                round_att(group_ended(s - FLIP_LAG - 4))
             if group_ended(s - FLIP_LAG - 6) is not None:
                 c, h = groups[group_ended(s - FLIP_LAG - 6)]
                 if c == CHUNKS - 1 and h == HEADS - 2:

@@ -243,7 +243,7 @@ def tile_jtransformer_b_kernel(
                     ALU.min,
                     accum_out=neg_max[:, i : i + 1],
                 )
-            exps[g, u] = work.tile([P, N], F32, name="exps", bufs=3)
+            exps[g, u] = work.tile([P, N], F32, name="exps", bufs=4)
             exp_sum[g, u] = small.tile([P, 1], F32, name="exp_sum")
             nc.scalar.activation(
                 exps[g, u][:, 0:keys],
@@ -259,7 +259,7 @@ def tile_jtransformer_b_kernel(
             keys = (c * BLOCKS_PER_CHUNK + u + 1) * P
             inv_sum = small.tile([P, 1], F32, name="inv_sum")
             nc.vector.reciprocal(inv_sum[:], exp_sum[g, u][:])
-            probs[g, u] = work.tile([P, N], BF16, name="probs", bufs=4)
+            probs[g, u] = work.tile([P, N], BF16, name="probs", bufs=5)
             nc.vector.tensor_scalar(
                 probs[g, u][:, 0:keys], exps[g, u][:, 0:keys], inv_sum[:], None, ALU.mult
             )
@@ -326,7 +326,8 @@ def tile_jtransformer_b_kernel(
         project_qk(0, 0)
 
         n_units = len(groups) * BLOCKS_PER_CHUNK
-        FLIP_LAG = 3
+        DIVIDE_LAG = 2
+        FLIP_LAG = 5
 
         def group_ended(s):
             if 0 <= s < n_units and s % BLOCKS_PER_CHUNK == BLOCKS_PER_CHUNK - 1:
@@ -339,8 +340,8 @@ def tile_jtransformer_b_kernel(
                 exponentials(g, u)
                 if u == 0 and g + 1 < len(groups):
                     project_qk(*groups[g + 1])
-            if 0 <= s - 1 < n_units:
-                divide(*divmod(s - 1, BLOCKS_PER_CHUNK))
+            if 0 <= s - DIVIDE_LAG < n_units:
+                divide(*divmod(s - DIVIDE_LAG, BLOCKS_PER_CHUNK))
             if 0 <= s - FLIP_LAG < n_units:
                 flip(*divmod(s - FLIP_LAG, BLOCKS_PER_CHUNK))
             if group_ended(s - FLIP_LAG - 2) is not None:

@@ -67,18 +67,14 @@ def tile_jtransformer_b_kernel(
         pos_sb = [held.tile([P, N], F32, name=f"pos_sb{b}") for b in range(CHANNEL_BLOCKS)]
         for b in range(CHANNEL_BLOCKS):
             nc.sync.dma_start(table[b][:], embed[block(b), :])
-            nc.sync.dma_start(pos_sb[b][:, 0:P], pos[block(b), 0:P])
-        for b in range(CHANNEL_BLOCKS):
-            nc.sync.dma_start(pos_sb[b][:, P:CHUNK], pos[block(b), P:CHUNK])
+            nc.sync.dma_start(pos_sb[b][:, 0:CHUNK], pos[block(b), 0:CHUNK])
         w_attn_sb = [held.tile([P, 3 * D], BF16, name=f"w_attn_sb{b}") for b in range(CHANNEL_BLOCKS)]
         for b in range(CHANNEL_BLOCKS):
-            nc.sync.dma_start(w_attn_sb[b][:, 2 * D : 3 * D], w_attn[block(b), 2 * D : 3 * D])
+            nc.sync.dma_start(w_attn_sb[b][:], w_attn[block(b), :])
         b_v_all = held.tile([P, D], F32, name="b_v_all")
         nc.sync.dma_start(
             b_v_all[:], b_attn[2 * D : 3 * D, :].rearrange("e o -> (e o)").partition_broadcast(P)
         )
-        for b in range(CHANNEL_BLOCKS):
-            nc.sync.dma_start(w_attn_sb[b][:, 0 : 2 * D], w_attn[block(b), 0 : 2 * D])
         for b in range(CHANNEL_BLOCKS):
             nc.sync.dma_start(pos_sb[b][:, CHUNK:N], pos[block(b), CHUNK:N])
         w_o_sb = [held.tile([P, D], BF16, name=f"w_o_sb{b}") for b in range(CHANNEL_BLOCKS)]
@@ -114,11 +110,11 @@ def tile_jtransformer_b_kernel(
         v_t = [held.tile([P, D], BF16, name=f"v_t{tb}") for tb in range(N // P)]
         att = [held.tile([P, N], BF16, name=f"att{h}") for h in range(HEADS)]
 
-        def look_up(b, first, count):
-            tokens = slice(first, first + count)
-            piece = offsets[:, first // 16 : (first + count) // 16]
+        def look_up(c, b):
+            chunk = slice(c * CHUNK, (c + 1) * CHUNK)
+            piece = offsets[:, c * CHUNK // 16 : (c + 1) * CHUNK // 16]
             nc.vector.tensor_tensor(
-                res[b][:, tokens], table[b][:].indirect(piece), pos_sb[b][:, tokens], ALU.add
+                res[b][:, chunk], table[b][:].indirect(piece), pos_sb[b][:, chunk], ALU.add
             )
 
         res_t = {}
@@ -189,21 +185,21 @@ def tile_jtransformer_b_kernel(
                 if 0 <= i - behind < BLOCKS_PER_CHUNK:
                     stage(first + i - behind)
 
-        def project_qk(c, h):
+        def project_qk(c, h, is_k):
             chunk = slice(c * CHUNK, (c + 1) * CHUNK)
-            for dest, m in ((q[h], h), (k[h], HEADS + h)):
-                product = product_banks.tile([P, CHUNK], F32, name="qk_ps", tag="product")
-                for b in range(CHANNEL_BLOCKS):
-                    nc.tensor.matmul(
-                        product[:],
-                        w_attn_sb[b][:, block(m)],
-                        x[b][:, chunk],
-                        start=(b == 0),
-                        stop=(b == CHANNEL_BLOCKS - 1),
-                    )
-                nc.scalar.activation(
-                    dest[:, chunk], product[:], FUNC.Identity, bias=column(ROW_B_QK + m)
+            dest, m = (k[h], HEADS + h) if is_k else (q[h], h)
+            product = product_banks.tile([P, CHUNK], F32, name="qk_ps", tag="product")
+            for b in range(CHANNEL_BLOCKS):
+                nc.tensor.matmul(
+                    product[:],
+                    w_attn_sb[b][:, block(m)],
+                    x[b][:, chunk],
+                    start=(b == 0),
+                    stop=(b == CHANNEL_BLOCKS - 1),
                 )
+            nc.scalar.activation(
+                dest[:, chunk], product[:], FUNC.Identity, bias=column(ROW_B_QK + m)
+            )
 
         groups = [(c, h) for c in range(CHUNKS) for h in range(HEADS)]
         exps = {}
@@ -297,9 +293,9 @@ def tile_jtransformer_b_kernel(
 
         out_ps = {}
 
-        def project_out(c, heads):
+        def project_out(c, heads, channel_blocks):
             chunk = slice(c * CHUNK, (c + 1) * CHUNK)
-            for m in range(CHANNEL_BLOCKS):
+            for m in channel_blocks:
                 if heads[0] == 0:
                     out_ps[c, m] = token_banks.tile([P, CHUNK], F32, name="out_ps", tag="bank")
                 for h in heads:
@@ -317,13 +313,12 @@ def tile_jtransformer_b_kernel(
                     )
                     nc.sync.dma_start(out[block(m), chunk], out_sb[:])
 
-        for i in range(-1, PREPARE_STEPS):
-            if i + 1 < BLOCKS_PER_CHUNK:
-                for b in range(CHANNEL_BLOCKS):
-                    look_up(b, (i + 1) * P, P)
-            if i >= 0:
-                prepare(0, i)
-        project_qk(0, 0)
+        for b in range(CHANNEL_BLOCKS):
+            look_up(0, b)
+        for i in range(PREPARE_STEPS):
+            prepare(0, i)
+        project_qk(0, 0, False)
+        project_qk(0, 0, True)
 
         n_units = len(groups) * BLOCKS_PER_CHUNK
         DIVIDE_LAG = 2
@@ -338,8 +333,10 @@ def tile_jtransformer_b_kernel(
             if s < n_units:
                 g, u = divmod(s, BLOCKS_PER_CHUNK)
                 exponentials(g, u)
-                if u == 0 and g + 1 < len(groups):
-                    project_qk(*groups[g + 1])
+                if g + 1 == len(groups):
+                    project_out(0, list(range(HEADS)), [u])
+                elif u < 2:
+                    project_qk(*groups[g + 1], u == 1)
             if 0 <= s - DIVIDE_LAG < n_units:
                 divide(*divmod(s - DIVIDE_LAG, BLOCKS_PER_CHUNK))
             if 0 <= s - FLIP_LAG < n_units:
@@ -351,12 +348,10 @@ def tile_jtransformer_b_kernel(
             if group_ended(s - FLIP_LAG - 6) is not None:
                 c, h = groups[group_ended(s - FLIP_LAG - 6)]
                 if c == CHUNKS - 1 and h == HEADS - 2:
-                    project_out(c, list(range(HEADS - 1)))
+                    project_out(c, list(range(HEADS - 1)), range(CHANNEL_BLOCKS))
                 elif c == CHUNKS - 1 and h == HEADS - 1:
-                    project_out(c, [HEADS - 1])
-                elif h == HEADS - 1:
-                    project_out(c, list(range(HEADS)))
+                    project_out(c, [HEADS - 1], range(CHANNEL_BLOCKS))
             if s < CHANNEL_BLOCKS:
-                look_up(s, CHUNK, CHUNK)
+                look_up(1, s)
             elif s - CHANNEL_BLOCKS < PREPARE_STEPS:
                 prepare(1, s - CHANNEL_BLOCKS)

import math
from contextlib import ExitStack

import concourse.mybir as mybir
from concourse.masks import make_identity

F32 = mybir.dt.float32
BF16 = mybir.dt.bfloat16
U16 = mybir.dt.uint16
I32 = mybir.dt.int32
ALU = mybir.AluOpType
FUNC = mybir.ActivationFunctionType

P = 128
D = 512
S = 2048
N = 1024
HEADS = 4
EPS = 1e-5
CHANNEL_BLOCKS = D // P
CHUNK = 512
CHUNKS = N // CHUNK
BLOCKS_PER_CHUNK = CHUNK // P
SCORE_SCALE = 1.0 / math.sqrt(P)
MASKED = -1.0e30

ROW_LN_W = 0
ROW_LN_B = ROW_LN_W + CHANNEL_BLOCKS
ROW_B_O = ROW_LN_B + CHANNEL_BLOCKS
ROW_B_QK = ROW_B_O + CHANNEL_BLOCKS
ROWS_USED = ROW_B_QK + 2 * CHANNEL_BLOCKS

FLOPS = 2 * D * 3 * D * N + 2 * D * D * N + 2 * (2 * D * N * (N + 1) // 2)


def block(i):
    return slice(i * P, (i + 1) * P)


def tile_jtransformer_b_kernel(
    tc, embed, pos, ln_w, ln_b, w_attn, b_attn, w_o, b_o, offs, out
):
    nc = tc.nc
    with ExitStack() as stack:
        held = stack.enter_context(tc.tile_pool(name="held", bufs=1))
        work = stack.enter_context(tc.tile_pool(name="work", bufs=2))
        small = stack.enter_context(tc.tile_pool(name="small", bufs=4))
        token_banks = stack.enter_context(tc.psum_pool(name="token_banks", bufs=4))
        flip_banks = stack.enter_context(tc.psum_pool(name="flip_banks", bufs=2))
        product_banks = stack.enter_context(tc.psum_pool(name="product_banks", bufs=2))

        offsets = held.tile([P, N // 16], U16, name="offsets")
        nc.sync.dma_start(offsets[:], offs)

        rows = held.tile([P, P], F32, name="rows")
        nc.gpsimd.memset(rows[:], 0.0)
        for first_row, vector in (
            (ROW_LN_W, ln_w),
            (ROW_LN_B, ln_b),
            (ROW_B_O, b_o),
            (ROW_B_QK, b_attn[0 : 2 * D, :]),
        ):
            as_rows = vector.rearrange("(r c) o -> r (c o)", c=P)
            nc.scalar.dma_start(rows[first_row : first_row + as_rows.shape[0], :], as_rows)

        table = [held.tile([P, S], F32, name=f"table{b}") for b in range(CHANNEL_BLOCKS)]
        pos_sb = [held.tile([P, N], F32, name=f"pos_sb{b}") for b in range(CHANNEL_BLOCKS)]
        for b in range(CHANNEL_BLOCKS):
            nc.sync.dma_start(table[b][:], embed[block(b), :])
            nc.sync.dma_start(pos_sb[b][:, 0:CHUNK], pos[block(b), 0:CHUNK])
        w_attn_sb = [held.tile([P, 3 * D], BF16, name=f"w_attn_sb{b}") for b in range(CHANNEL_BLOCKS)]
        for b in range(CHANNEL_BLOCKS):
            nc.sync.dma_start(w_attn_sb[b][:], w_attn[block(b), :])
        b_v_all = held.tile([P, D], F32, name="b_v_all")
        nc.sync.dma_start(
            b_v_all[:], b_attn[2 * D : 3 * D, :].rearrange("e o -> (e o)").partition_broadcast(P)
        )
        for b in range(CHANNEL_BLOCKS):
            nc.sync.dma_start(pos_sb[b][:, CHUNK:N], pos[block(b), CHUNK:N])
        w_o_sb = [held.tile([P, D], BF16, name=f"w_o_sb{b}") for b in range(CHANNEL_BLOCKS)]
        for b in range(CHANNEL_BLOCKS):
            nc.sync.dma_start(w_o_sb[b][:], w_o[block(b), :])

        ident_f32 = held.tile([P, P], F32, name="ident_f32")
        make_identity(nc, ident_f32[:])
        ident_bf16 = held.tile([P, P], BF16, name="ident_bf16")
        make_identity(nc, ident_bf16[:])
        key_minus_query = held.tile([P, P], I32, name="key_minus_query")
        nc.gpsimd.iota(key_minus_query[:], pattern=[[1, P]], base=0, channel_multiplier=-1)
        causal = held.tile([P, P], BF16, name="causal")
        nc.vector.tensor_scalar(causal[:], key_minus_query[:], 0.0, MASKED, ALU.is_gt, ALU.mult)

        half = held.tile([P, 1], F32, name="half")
        nc.gpsimd.memset(half[:], 0.5)
        warmed = held.tile([P, 1], F32, name="warmed")
        nc.scalar.activation(warmed[:], half[:], FUNC.Exp)

        columns_ps = flip_banks.tile([P, P], F32, name="columns_ps", tag="flip")
        nc.tensor.transpose(columns_ps[:], rows[:], ident_f32[:])
        columns = held.tile([P, ROWS_USED], F32, name="columns")
        nc.vector.tensor_copy(columns[:], columns_ps[:, 0:ROWS_USED])

        def column(row):
            return columns[:, row : row + 1]

        res = [held.tile([P, N], F32, name=f"res{b}") for b in range(CHANNEL_BLOCKS)]
        x = [held.tile([P, N], BF16, name=f"x{b}") for b in range(CHANNEL_BLOCKS)]
        q = [held.tile([P, N], BF16, name=f"q{h}") for h in range(HEADS)]
        k = [held.tile([P, N], BF16, name=f"k{h}") for h in range(HEADS)]
        v_t = [held.tile([P, D], BF16, name=f"v_t{tb}") for tb in range(N // P)]
        att = [held.tile([P, N], BF16, name=f"att{h}") for h in range(HEADS)]

        def look_up(c, b):
            chunk = slice(c * CHUNK, (c + 1) * CHUNK)
            piece = offsets[:, c * CHUNK // 16 : (c + 1) * CHUNK // 16]
            nc.vector.tensor_tensor(
                res[b][:, chunk], table[b][:].indirect(piece), pos_sb[b][:, chunk], ALU.add
            )

        res_t = {}
        mean_var = {}
        sd = {}
        normed_t = {}

        def moments(tb):
            res_t[tb] = token_banks.tile([P, D], F32, name="res_t", tag="bank")
            for b in range(CHANNEL_BLOCKS):
                nc.tensor.transpose(res_t[tb][:, block(b)], res[b][:, block(tb)], ident_f32[:])
            stats = small.tile([P, 6], F32, name="stats")
            nc.vector.bn_stats(stats[:], res_t[tb][:])
            mean_var[tb] = small.tile([P, 2], F32, name="mean_var")
            nc.vector.bn_aggr(mean_var[tb][:], stats[:])
            sd[tb] = small.tile([P, 1], F32, name="sd")
            nc.gpsimd.tensor_tensor(sd[tb][:], mean_var[tb][:, 1:2], half[:], ALU.pow)

        def normalise(tb):
            sd_eps = small.tile([P, 1], F32, name="sd_eps")
            nc.vector.tensor_scalar_add(sd_eps[:], sd[tb][:], EPS)
            inv_sd = small.tile([P, 1], F32, name="inv_sd")
            nc.vector.reciprocal(inv_sd[:], sd_eps[:])
            normed_t[tb] = work.tile([P, D], F32, name="normed_t", bufs=4)
            if tb < BLOCKS_PER_CHUNK:
                minus_mean = small.tile([P, 1], F32, name="minus_mean")
                nc.vector.tensor_scalar(
                    minus_mean[:], mean_var[tb][:, 0:1], inv_sd[:], -1.0, ALU.mult, ALU.mult
                )
                nc.scalar.activation(
                    normed_t[tb][:], res_t[tb][:], FUNC.Identity, bias=minus_mean[:], scale=inv_sd[:]
                )
            else:
                nc.vector.tensor_scalar(
                    normed_t[tb][:], res_t[tb][:], mean_var[tb][:, 0:1], inv_sd[:], ALU.subtract, ALU.mult
                )

        def flip_back(tb):
            normed_ps = flip_banks.tile([P, CHANNEL_BLOCKS, P], F32, name="normed_ps", tag="flip")
            for b in range(CHANNEL_BLOCKS):
                nc.tensor.transpose(normed_ps[:, b, :], normed_t[tb][:, block(b)], ident_f32[:])
            for b in range(CHANNEL_BLOCKS):
                nc.scalar.activation(
                    x[b][:, block(tb)],
                    normed_ps[:, b, :],
                    FUNC.Identity,
                    bias=column(ROW_LN_B + b),
                    scale=column(ROW_LN_W + b),
                )

        def project_v(tb):
            product = product_banks.tile([P, D], F32, name="v_ps", tag="product")
            for b in range(CHANNEL_BLOCKS):
                nc.tensor.matmul(
                    product[:],
                    x[b][:, block(tb)],
                    w_attn_sb[b][:, 2 * D : 3 * D],
                    start=(b == 0),
                    stop=(b == CHANNEL_BLOCKS - 1),
                )
            nc.vector.tensor_tensor(v_t[tb][:], product[:], b_v_all[:], ALU.add)

        PREPARE_STEPS = BLOCKS_PER_CHUNK + 5

        def prepare(c, i):
            first = c * BLOCKS_PER_CHUNK
            for behind, stage in ((0, moments), (1, normalise), (3, flip_back), (5, project_v)):
                if 0 <= i - behind < BLOCKS_PER_CHUNK:
                    stage(first + i - behind)

        def project_qk(c, h, is_k):
            chunk = slice(c * CHUNK, (c + 1) * CHUNK)
            dest, m = (k[h], HEADS + h) if is_k else (q[h], h)
            product = product_banks.tile([P, CHUNK], F32, name="qk_ps", tag="product")
            for b in range(CHANNEL_BLOCKS):
                nc.tensor.matmul(
                    product[:],
                    w_attn_sb[b][:, block(m)],
                    x[b][:, chunk],
                    start=(b == 0),
                    stop=(b == CHANNEL_BLOCKS - 1),
                )
            nc.scalar.activation(
                dest[:, chunk], product[:], FUNC.Identity, bias=column(ROW_B_QK + m)
            )

        groups = [(c, h) for c in range(CHUNKS) for h in range(HEADS)]
        exps = {}
        exp_sum = {}
        probs = {}
        probs_t = {}
        weighted = {}

        def exponentials(g, u):
            c, h = groups[g]
            n_banks = c + 1
            jb = c * BLOCKS_PER_CHUNK + u
            keys = (jb + 1) * P
            widths = [min(CHUNK, keys - i * CHUNK) for i in range(n_banks)]
            neg_scores = work.tile([P, N], F32, name="neg_scores", bufs=3)
            neg_max = small.tile([P, n_banks], F32, name="neg_max")
            for i, width in enumerate(widths):
                bank = token_banks.tile([P, CHUNK], F32, name="scores", tag="bank")
                diagonal = i == n_banks - 1
                nc.tensor.matmul(
                    bank[:, 0:width],
                    q[h][:, block(jb)],
                    k[h][:, i * CHUNK : i * CHUNK + width],
                    start=True,
                    stop=not diagonal,
                )
                if diagonal:
                    nc.tensor.matmul(
                        bank[:, width - P : width], ident_bf16[:], causal[:], start=False, stop=True
                    )
                nc.vector.tensor_scalar(
                    neg_scores[:, i * CHUNK : i * CHUNK + width],
                    bank[:, 0:width],
                    -SCORE_SCALE,
                    None if i == 0 else neg_max[:, i - 1 : i],
                    ALU.mult,
                    ALU.min,
                    accum_out=neg_max[:, i : i + 1],
                )
            exps[g, u] = work.tile([P, N], F32, name="exps", bufs=4)
            exp_sum[g, u] = small.tile([P, 1], F32, name="exp_sum")
            nc.scalar.activation(
                exps[g, u][:, 0:keys],
                neg_scores[:, 0:keys],
                FUNC.Exp,
                bias=neg_max[:, n_banks - 1 : n_banks],
                scale=-1.0,
                accum_out=exp_sum[g, u][:],
            )

        def divide(g, u):
            c, h = groups[g]
            keys = (c * BLOCKS_PER_CHUNK + u + 1) * P
            inv_sum = small.tile([P, 1], F32, name="inv_sum")
            nc.vector.reciprocal(inv_sum[:], exp_sum[g, u][:])
            probs[g, u] = work.tile([P, N], BF16, name="probs", bufs=5)
            nc.vector.tensor_scalar(
                probs[g, u][:, 0:keys], exps[g, u][:, 0:keys], inv_sum[:], None, ALU.mult
            )

        def flip(g, u):
            c, h = groups[g]
            if u == 0:
                probs_t[g] = work.tile([P, (c + 1) * BLOCKS_PER_CHUNK, CHUNK], BF16, name="probs_t")
            jb = c * BLOCKS_PER_CHUNK + u
            flipped = flip_banks.tile([P, N], BF16, name="probs_ps", tag="flip")
            for tb in range(jb + 1):
                nc.tensor.transpose(flipped[:, block(tb)], probs[g, u][:, block(tb)], ident_bf16[:])
            nc.scalar.copy(
                probs_t[g][:, 0 : jb + 1, block(u)],
                flipped[:, 0 : (jb + 1) * P].rearrange("p (tb j) -> p tb j", j=P),
            )

        def weighted_sum(g):
            c, h = groups[g]
            key_blocks = (c + 1) * BLOCKS_PER_CHUNK
            weighted[g] = product_banks.tile([P, CHUNK], F32, name="weighted", tag="product")
            for tb in range(key_blocks):
                first = max(0, tb - c * BLOCKS_PER_CHUNK) * P
                nc.tensor.matmul(
                    weighted[g][:, first:CHUNK],
                    v_t[tb][:, block(h)],
                    probs_t[g][:, tb, first:CHUNK],
                    start=(tb == 0),
                    stop=(tb == key_blocks - 1),
                )

        def round_att(g):
            c, h = groups[g]
            nc.scalar.copy(att[h][:, c * CHUNK : (c + 1) * CHUNK], weighted[g][:])

        out_ps = {}

        def project_out(c, heads, channel_blocks):
            chunk = slice(c * CHUNK, (c + 1) * CHUNK)
            for m in channel_blocks:
                if heads[0] == 0:
                    out_ps[c, m] = token_banks.tile([P, CHUNK], F32, name="out_ps", tag="bank")
                for h in heads:
                    nc.tensor.matmul(
                        out_ps[c, m][:],
                        w_o_sb[h][:, block(m)],
                        att[h][:, chunk],
                        start=(h == 0),
                        stop=(h == HEADS - 1),
                    )
                if heads[-1] == HEADS - 1:
                    out_sb = work.tile([P, CHUNK], F32, name="out_sb", bufs=CHANNEL_BLOCKS)
                    nc.vector.scalar_tensor_tensor(
                        out_sb[:], out_ps[c, m][:], column(ROW_B_O + m), res[m][:, chunk], ALU.add, ALU.add
                    )
                    nc.sync.dma_start(out[block(m), chunk], out_sb[:])

        for b in range(CHANNEL_BLOCKS):
            look_up(0, b)
        for i in range(PREPARE_STEPS):
            prepare(0, i)
        project_qk(0, 0, False)
        project_qk(0, 0, True)

        n_units = len(groups) * BLOCKS_PER_CHUNK
        DIVIDE_LAG = 2
        FLIP_LAG = 5

        def group_ended(s):
            if 0 <= s < n_units and s % BLOCKS_PER_CHUNK == BLOCKS_PER_CHUNK - 1:
                return s // BLOCKS_PER_CHUNK
            return None

        for s in range(n_units + FLIP_LAG + 7):
            if s < n_units:
                g, u = divmod(s, BLOCKS_PER_CHUNK)
                exponentials(g, u)
                if g + 1 == len(groups):
                    project_out(0, list(range(HEADS)), [u])
                elif u < 2:
                    project_qk(*groups[g + 1], u == 1)
            if 0 <= s - DIVIDE_LAG < n_units:
                divide(*divmod(s - DIVIDE_LAG, BLOCKS_PER_CHUNK))
            if 0 <= s - FLIP_LAG < n_units:
                flip(*divmod(s - FLIP_LAG, BLOCKS_PER_CHUNK))
            if group_ended(s - FLIP_LAG - 2) is not None:
                weighted_sum(group_ended(s - FLIP_LAG - 2))
            if group_ended(s - FLIP_LAG - 4) is not None:
                round_att(group_ended(s - FLIP_LAG - 4))
            if group_ended(s - FLIP_LAG - 6) is not None:
                c, h = groups[group_ended(s - FLIP_LAG - 6)]
                if c == CHUNKS - 1 and h == HEADS - 2:
                    project_out(c, list(range(HEADS - 1)), range(CHANNEL_BLOCKS))
                elif c == CHUNKS - 1 and h == HEADS - 1:
                    project_out(c, [HEADS - 1], range(CHANNEL_BLOCKS))
            if s < CHANNEL_BLOCKS:
                look_up(1, s)
            elif s - CHANNEL_BLOCKS < PREPARE_STEPS:
                prepare(1, s - CHANNEL_BLOCKS)
